import numpy as np
import ml_dtypes


def mxq(x, axis, fmt="e4m3"):
    dtype, down = {"e4m3": (ml_dtypes.float8_e4m3fn, 7), "e5m2": (ml_dtypes.float8_e5m2, 14)}[fmt]
    v = np.moveaxis(np.asarray(x, np.float32).astype(ml_dtypes.bfloat16).astype(np.float64), axis, -1)
    blocks = v.reshape(v.shape[:-1] + (-1, 32))
    amax = np.abs(blocks).max(-1, keepdims=True)
    byte = np.maximum(np.where(amax > 0, np.frexp(amax)[1] - 1 + 127, 0) - down, 1)
    scale = np.exp2(byte - 127.0)
    codes = (blocks / scale).astype(np.float32).astype(dtype).astype(np.float64)
    return np.moveaxis((codes * scale).reshape(v.shape), -1, axis)


WIDE = False


def mx_kscale(k):
    if not WIDE:
        return np.ones(k)
    levels = np.array([10, -10, 5, -5, 0])
    a = np.random.permutation(np.resize(levels, k // 512 * 4)).reshape(k // 512, 4)
    idx = np.arange(k)
    return np.exp2(a[idx // 512, idx % 128 // 32])


BF16 = ml_dtypes.bfloat16


def bf(x):
    return np.asarray(x, np.float32).astype(BF16)


def f64(x):
    return np.asarray(x).astype(np.float64)


E2M1 = np.array([0.0, 0.5, 1.0, 1.5, 2.0, 3.0, 4.0, 6.0, -0.0, -0.5, -1.0, -1.5, -2.0, -3.0, -4.0, -6.0])


def pack_weight(w, fmt):
    k, n = w.shape
    w = f64(bf(w)).reshape(k // 32, 32, n)
    amax = np.abs(w).max(1)
    if fmt == "e4m3":
        byte = np.frexp(amax)[1] - 1 + 127 - 7
    else:
        mant, ex = np.frexp(amax / 6.0)
        byte = np.where(mant > 0.5, ex, ex - 1) + 127
    byte = np.clip(np.where(amax > 0, byte, 1), 1, 254)
    scaled = (w * np.exp2(127.0 - byte)[:, None, :]).reshape(k, n).astype(np.float32)
    by_word = np.ascontiguousarray(scaled.reshape(k // 512, 128, 4, n).transpose(0, 1, 3, 2))
    if fmt == "e4m3":
        words = by_word.astype(ml_dtypes.float8_e4m3fn).view(np.uint8)
    else:
        c = by_word.astype(ml_dtypes.float4_e2m1fn).view(np.uint8) & 0xF
        words = c[..., 0::2] | (c[..., 1::2] << 4)
    return np.ascontiguousarray(words), np.ascontiguousarray(byte.astype(np.uint8).reshape(k // 512, 16, n))


def unpack_weight(words, scales, fmt):
    g, p, n, _ = words.shape
    if fmt == "e4m3":
        vals = np.ascontiguousarray(words).view(ml_dtypes.float8_e4m3fn).astype(np.float64)
    else:
        nib = np.empty((g, p, n, 4), np.uint8)
        nib[..., 0::2] = words & 0xF
        nib[..., 1::2] = words >> 4
        vals = E2M1[nib]
    vals = vals * np.repeat(np.exp2(scales.astype(np.float64) - 127.0), 8, axis=1)[..., None]
    return vals.transpose(0, 1, 3, 2).reshape(g * 512, n)

def pack4(w):
    words, scales = pack_weight(w, "e2m1")
    return words.reshape(words.shape[0], 128, -1), scales


def unpack4(words, scales):
    return unpack_weight(words.reshape(words.shape[0], 128, -1, 2), scales, "e2m1")


B, N, HID, H, D = 2, 128, 2048, 16, 128


def apply_rope(t, rope):
    freqs = rope[:, 0, :]
    cos = np.repeat(freqs[:, 0::2], 2, axis=-1)[None, None]
    sin = np.repeat(freqs[:, 1::2], 2, axis=-1)[None, None]
    tr = t.reshape(*t.shape[:-1], -1, 2)
    t_real, t_imag = tr[..., 0], tr[..., 1]
    t_rot = np.stack([-t_imag, t_real], axis=-1).reshape(t.shape)
    return t * cos + t_rot * sin


def setup_inputs():
    s = mx_kscale(HID)
    x = bf(np.random.standard_normal((B, N, HID)) * s)
    rope = bf(np.random.uniform(size=(N, 1, D)))
    words, scales = pack4(np.random.standard_normal((HID, 3 * H * D)) * 1.5 / np.sqrt(HID) / s[:, None])
    return {"x": x,
            "rope": rope,
            "qkv_w_words": words,
            "qkv_w_scales": scales}


def reference(x, rope, qkv_w_words, qkv_w_scales):
    r = f64(rope)
    qkv = (mxq(f64(x), 2, "e4m3") @ unpack4(qkv_w_words, qkv_w_scales)).reshape(B, N, 3, H, D)
    q = np.transpose(qkv[:, :, 0], (0, 2, 1, 3))
    k = np.transpose(qkv[:, :, 1], (0, 2, 1, 3))
    v = np.transpose(qkv[:, :, 2], (0, 2, 1, 3))
    return apply_rope(q, r), apply_rope(k, r), v

@@ -1,0 +1,172 @@
+from contextlib import ExitStack
+
+import concourse.mybir as mybir
+from concourse.masks import make_identity
+
+F32 = mybir.dt.float32
+BF16 = mybir.dt.bfloat16
+I32 = mybir.dt.int32
+U32 = mybir.dt.uint32
+U8 = mybir.dt.uint8
+FP8X4 = mybir.dt.float8_e4m3fn_x4
+FP4X4 = mybir.dt.float4_e2m1fn_x4
+MULT = mybir.AluOpType.mult
+ADD = mybir.AluOpType.add
+
+P = 128
+BATCH = 2
+POSITIONS = 128
+HID = 2048
+HEADS = 16
+D = 128
+PAIRS = D // 2
+COMPONENTS = 3
+COMPONENT_COLS = HEADS * D
+
+PACK = 4
+K_PASS = P * PACK
+PASSES = HID // K_PASS
+
+BANK_COLS = 512
+BANK_HEADS = BANK_COLS // D
+BANKS_PER_COMPONENT = COMPONENT_COLS // BANK_COLS
+SLAB_COLS = 1024
+SLABS_PER_COMPONENT = COMPONENT_COLS // SLAB_COLS
+PARITIES = 2
+
+FLOPS = 2 * BATCH * POSITIONS * HID * COMPONENTS * COMPONENT_COLS
+
+
+def tile_attention_pa_kernel(tc, x, rope, qkv_w_words, qkv_w_scales, out_0, out_1, out_2):
+    nc = tc.nc
+    outs = [out_0, out_1, out_2]
+
+    with ExitStack() as ctx:
+        keep = ctx.enter_context(tc.tile_pool(name="keep", bufs=1))
+        work = ctx.enter_context(tc.tile_pool(name="work", bufs=3))
+        psum = ctx.enter_context(tc.psum_pool(name="psum", bufs=8))
+        ctx.enter_context(tc.manual_schedule())
+
+        planes = []
+        for c in range(COMPONENTS):
+            plane = keep.tile([P, PASSES, COMPONENT_COLS], U8, align_bytes=64, name="plane%d" % c)
+            nc.vector.memset(plane[:].bitcast(I32), 0)
+            planes.append(plane)
+
+        identity = keep.tile([P, P], F32, name="identity")
+        make_identity(nc, identity[:])
+
+        x_sb = keep.tile([P, PARITIES, HID], BF16, name="x_sb")
+        x_by_parity = x.rearrange("b (m par) k -> par m b k", par=PARITIES)
+        for par in range(PARITIES):
+            nc.sync.dma_start(out=x_sb[:, par, :], in_=x_by_parity[par])
+
+        rope_sb = keep.tile([P, PARITIES, D], BF16, name="rope_sb")
+        rope_rows = rope.rearrange("(m par) o d -> m par (o d)", par=PARITIES)
+        for b in range(BATCH):
+            nc.scalar.dma_start(out=rope_sb[b:P:BATCH, :, :], in_=rope_rows)
+
+        slabs = []
+        for c in range(COMPONENTS):
+            cols = slice(c * COMPONENT_COLS, (c + 1) * COMPONENT_COLS)
+            for half in range(2):
+                for r in range(4):
+                    nc.sync.dma_start(
+                        out=planes[c][32 * half + r : P : 64, :, :].bitcast(I32),
+                        in_=qkv_w_scales[:, 4 * half + r : 16 : 8, cols].rearrange("g q n -> q g n").bitcast(I32),
+                    )
+            for s in range(SLABS_PER_COMPONENT):
+                first = c * COMPONENT_COLS + s * SLAB_COLS
+                slab = keep.tile([P, PASSES, 2 * SLAB_COLS], U8, align_bytes=64, name="slab%d_%d" % (c, s))
+                nc.sync.dma_start(
+                    out=slab[:].bitcast(I32),
+                    in_=qkv_w_words[:, :, 2 * first : 2 * (first + SLAB_COLS)].rearrange("g p n -> p g n").bitcast(I32),
+                )
+                slabs.append(slab)
+
+        x_codes = []
+        x_scales = []
+        grouped_tiles = []
+        for par in range(PARITIES):
+            x_words = x_sb[:, par, :].bitcast(F32)
+            grouped = keep.tile([P, PASSES * P * PACK], BF16, align_bytes=64, name="grouped%d" % par)
+            grouped_words = grouped[:].bitcast(F32).rearrange("p (g t u) -> p g t u", g=PASSES, u=2)
+            for pair in range(PASSES // 2):
+                xt = psum.tile([P, 2, 2, P], F32, tag="bank", name="xt")
+                for g2 in range(2):
+                    g = 2 * pair + g2
+                    for u in range(2):
+                        nc.tensor.transpose(
+                            xt[:, g2, u, :], x_words[:, 256 * g + u : 256 * (g + 1) : 2], identity[:]
+                        )
+                source = xt[:].rearrange("p g u t -> p g t u")
+                target = grouped_words[:, 2 * pair : 2 * pair + 2, :, :]
+                if pair == 0:
+                    nc.vector.tensor_copy(out=target, in_=source)
+                else:
+                    nc.scalar.copy(out=target, in_=source)
+            grouped_tiles.append(grouped)
+        for par in range(PARITIES):
+            codes = keep.tile([P, PASSES * P], U32, align_bytes=64, name="x_codes%d" % par)
+            scales = keep.tile([P, PASSES * P], U8, align_bytes=64, name="x_scales%d" % par)
+            nc.vector.quantize_mx(out=codes[:].bitcast(FP8X4), scales=scales[:], in_=grouped_tiles[par][:])
+            x_codes.append(codes)
+            x_scales.append(scales)
+
+        rope_pairs = rope_sb[:].rearrange("p par (j e) -> p par j e", e=2)
+        cos2 = keep.tile([P, PARITIES, PAIRS, 2], F32, name="cos2")
+        nc.vector.tensor_copy(out=cos2[:], in_=rope_pairs[:, :, :, 0:1].to_broadcast([P, PARITIES, PAIRS, 2]))
+        sin_pm = keep.tile([P, PARITIES, 2, PAIRS], F32, name="sin_pm")
+        nc.vector.tensor_scalar_mul(out=sin_pm[:, :, 0, :], in0=rope_pairs[:, :, :, 1], scalar1=-1.0)
+        nc.vector.tensor_copy(out=sin_pm[:, :, 1, :], in_=rope_pairs[:, :, :, 1])
+
+        for c in range(COMPONENTS):
+            for bank in range(BANKS_PER_COMPONENT):
+                col = bank * BANK_COLS
+                slab = slabs[c * SLABS_PER_COMPONENT + col // SLAB_COLS]
+                in_slab = col % SLAB_COLS
+                result = keep.tile([P, BANK_HEADS, PARITIES, D], F32, name="result%d_%d" % (c, bank))
+                for par in range(PARITIES):
+                    acc = psum.tile([P, BANK_COLS], F32, tag="bank", name="acc")
+                    for g in range(PASSES):
+                        nc.tensor.matmul_mx(
+                            out=acc[:],
+                            lhsT=x_codes[par][:, g * P : (g + 1) * P].bitcast(FP8X4),
+                            lhsT_scale=x_scales[par][:, g * P : (g + 1) * P],
+                            rhs=slab[:, g, 2 * in_slab : 2 * (in_slab + BANK_COLS)].bitcast(FP4X4),
+                            rhs_scale=planes[c][:, g, col : col + BANK_COLS],
+                            start=(g == 0),
+                            stop=(g == PASSES - 1),
+                        )
+                    by_head = acc[:].rearrange("p (h d) -> p h d", h=BANK_HEADS)
+                    if c == COMPONENTS - 1:
+                        nc.scalar.copy(out=result[:, :, par, :], in_=by_head)
+                    else:
+                        by_pair = acc[:].rearrange("p (h j e) -> p h j e", h=BANK_HEADS, e=2)
+                        straight = work.tile([P, BANK_HEADS, D], F32, name="straight")
+                        nc.vector.tensor_tensor(
+                            out=straight[:],
+                            in0=by_head,
+                            in1=cos2[:, par, :, :].rearrange("p j e -> p (j e)").unsqueeze(1).to_broadcast([P, BANK_HEADS, D]),
+                            op=MULT,
+                        )
+                        crossed = work.tile([P, 2, BANK_HEADS, PAIRS], F32, name="crossed")
+                        for e in range(2):
+                            nc.vector.tensor_tensor(
+                                out=crossed[:, e, :, :],
+                                in0=by_pair[:, :, :, 1 - e],
+                                in1=sin_pm[:, par, e, :].unsqueeze(1).to_broadcast([P, BANK_HEADS, PAIRS]),
+                                op=MULT,
+                            )
+                        nc.gpsimd.tensor_tensor(
+                            out=result[:, :, par, :].rearrange("p h (j e) -> p h j e", e=2),
+                            in0=straight[:].rearrange("p h (j e) -> p h j e", e=2),
+                            in1=crossed[:].rearrange("p e h j -> p h j e"),
+                            op=ADD,
+                        )
+                for h in range(BANK_HEADS):
+                    head = bank * BANK_HEADS + h
+                    nc.sync.dma_start(
+                        out=outs[c][:, head, :, :].rearrange("b (m par) d -> m b (par d)", par=PARITIES),
+                        in_=result[:, h, :, :].rearrange("p par d -> p (par d)"),
+                    )

@@ -21,6 +21,7 @@ HEADS = 16
 D = 128
 PAIRS = D // 2
 COMPONENTS = 3
+Q, K, V = range(COMPONENTS)
 COMPONENT_COLS = HEADS * D
 
 PACK = 4
@@ -29,9 +30,7 @@ PASSES = HID // K_PASS
 
 BANK_COLS = 512
 BANK_HEADS = BANK_COLS // D
-BANKS_PER_COMPONENT = COMPONENT_COLS // BANK_COLS
-SLAB_COLS = 1024
-SLABS_PER_COMPONENT = COMPONENT_COLS // SLAB_COLS
+HALF = COMPONENT_COLS // 2
 PARITIES = 2
 
 FLOPS = 2 * BATCH * POSITIONS * HID * COMPONENTS * COMPONENT_COLS
@@ -47,126 +46,179 @@ def tile_attention_pa_kernel(tc, x, rope, qkv_w_words, qkv_w_scales, out_0, out_
         psum = ctx.enter_context(tc.psum_pool(name="psum", bufs=8))
         ctx.enter_context(tc.manual_schedule())
 
-        planes = []
-        for c in range(COMPONENTS):
-            plane = keep.tile([P, PASSES, COMPONENT_COLS], U8, align_bytes=64, name="plane%d" % c)
-            nc.vector.memset(plane[:].bitcast(I32), 0)
-            planes.append(plane)
+        v_first = (V, 0, HALF)
+        q_all = (Q, 0, COMPONENT_COLS)
+        k_all = (K, 0, COMPONENT_COLS)
+        v_last = (V, HALF, HALF)
+        groups = [v_first, q_all, k_all, v_last]
+
+        planes = {}
+        slabs = {}
+        for group in groups:
+            planes[group] = keep.tile([P, PASSES, group[2]], U8, align_bytes=64, name="plane%d_%d" % group[:2])
+            slabs[group] = keep.tile([P, PASSES, 2 * group[2]], U8, align_bytes=64, name="slab%d_%d" % group[:2])
 
         identity = keep.tile([P, P], F32, name="identity")
         make_identity(nc, identity[:])
-
-        x_sb = keep.tile([P, PARITIES, HID], BF16, name="x_sb")
-        x_by_parity = x.rearrange("b (m par) k -> par m b k", par=PARITIES)
-        for par in range(PARITIES):
-            nc.sync.dma_start(out=x_sb[:, par, :], in_=x_by_parity[par])
+        nc.vector.memset(planes[v_first][:].bitcast(I32), 0)
+        nc.gpsimd.memset(planes[q_all][:].bitcast(I32), 0)
+        nc.vector.memset(planes[k_all][:].bitcast(I32), 0)
 
         rope_sb = keep.tile([P, PARITIES, D], BF16, name="rope_sb")
         rope_rows = rope.rearrange("(m par) o d -> m par (o d)", par=PARITIES)
         for b in range(BATCH):
-            nc.scalar.dma_start(out=rope_sb[b:P:BATCH, :, :], in_=rope_rows)
+            nc.gpsimd.dma_start(out=rope_sb[b:P:BATCH, :, :], in_=rope_rows)
 
-        slabs = []
-        for c in range(COMPONENTS):
-            cols = slice(c * COMPONENT_COLS, (c + 1) * COMPONENT_COLS)
-            for half in range(2):
-                for r in range(4):
-                    nc.sync.dma_start(
-                        out=planes[c][32 * half + r : P : 64, :, :].bitcast(I32),
-                        in_=qkv_w_scales[:, 4 * half + r : 16 : 8, cols].rearrange("g q n -> q g n").bitcast(I32),
-                    )
-            for s in range(SLABS_PER_COMPONENT):
-                first = c * COMPONENT_COLS + s * SLAB_COLS
-                slab = keep.tile([P, PASSES, 2 * SLAB_COLS], U8, align_bytes=64, name="slab%d_%d" % (c, s))
+        x_by_parity = x.rearrange("b (m par) k -> par m b k", par=PARITIES)
+        x_sb = keep.tile([P, PARITIES, HID], BF16, name="x_sb")
+
+        def load_x(ks):
+            for par in range(PARITIES):
+                nc.sync.dma_start(out=x_sb[:, par, ks], in_=x_by_parity[par][:, :, ks])
+
+        def load_scales(group):
+            c, first, width = group
+            cols = slice(c * COMPONENT_COLS + first, c * COMPONENT_COLS + first + width)
+            for r in range(4):
                 nc.sync.dma_start(
-                    out=slab[:].bitcast(I32),
-                    in_=qkv_w_words[:, :, 2 * first : 2 * (first + SLAB_COLS)].rearrange("g p n -> p g n").bitcast(I32),
+                    out=planes[group][r:P:32, :, :].bitcast(I32),
+                    in_=qkv_w_scales[:, r:16:4, cols].rearrange("g q n -> q g n").bitcast(I32),
                 )
-                slabs.append(slab)
 
-        x_codes = []
-        x_scales = []
-        grouped_tiles = []
-        for par in range(PARITIES):
-            x_words = x_sb[:, par, :].bitcast(F32)
-            grouped = keep.tile([P, PASSES * P * PACK], BF16, align_bytes=64, name="grouped%d" % par)
-            grouped_words = grouped[:].bitcast(F32).rearrange("p (g t u) -> p g t u", g=PASSES, u=2)
-            for pair in range(PASSES // 2):
-                xt = psum.tile([P, 2, 2, P], F32, tag="bank", name="xt")
-                for g2 in range(2):
-                    g = 2 * pair + g2
-                    for u in range(2):
-                        nc.tensor.transpose(
-                            xt[:, g2, u, :], x_words[:, 256 * g + u : 256 * (g + 1) : 2], identity[:]
-                        )
-                source = xt[:].rearrange("p g u t -> p g t u")
-                target = grouped_words[:, 2 * pair : 2 * pair + 2, :, :]
-                if pair == 0:
-                    nc.vector.tensor_copy(out=target, in_=source)
-                else:
-                    nc.scalar.copy(out=target, in_=source)
-            grouped_tiles.append(grouped)
-        for par in range(PARITIES):
-            codes = keep.tile([P, PASSES * P], U32, align_bytes=64, name="x_codes%d" % par)
-            scales = keep.tile([P, PASSES * P], U8, align_bytes=64, name="x_scales%d" % par)
-            nc.vector.quantize_mx(out=codes[:].bitcast(FP8X4), scales=scales[:], in_=grouped_tiles[par][:])
-            x_codes.append(codes)
-            x_scales.append(scales)
+        def load_words(group, passes, cols):
+            c, first, width = group
+            base = 2 * (c * COMPONENT_COLS + first)
+            nc.sync.dma_start(
+                out=slabs[group][:, passes, 2 * cols.start : 2 * cols.stop].bitcast(I32),
+                in_=qkv_w_words[passes, :, base + 2 * cols.start : base + 2 * cols.stop]
+                .rearrange("g p n -> p g n")
+                .bitcast(I32),
+            )
+
+        every_pass = slice(0, PASSES)
+        load_x(slice(0, HID // 2))
+        load_scales(v_first)
+        load_words(v_first, slice(0, PASSES // 2), slice(0, HALF))
+        load_x(slice(HID // 2, HID))
+        load_words(v_first, slice(PASSES // 2, PASSES), slice(0, HALF))
+        load_scales(q_all)
+        load_words(q_all, every_pass, slice(0, HALF))
+        load_words(q_all, every_pass, slice(HALF, COMPONENT_COLS))
+        load_scales(k_all)
+        load_words(k_all, every_pass, slice(0, COMPONENT_COLS))
 
         rope_pairs = rope_sb[:].rearrange("p par (j e) -> p par j e", e=2)
         cos2 = keep.tile([P, PARITIES, PAIRS, 2], F32, name="cos2")
-        nc.vector.tensor_copy(out=cos2[:], in_=rope_pairs[:, :, :, 0:1].to_broadcast([P, PARITIES, PAIRS, 2]))
-        sin_pm = keep.tile([P, PARITIES, 2, PAIRS], F32, name="sin_pm")
-        nc.vector.tensor_scalar_mul(out=sin_pm[:, :, 0, :], in0=rope_pairs[:, :, :, 1], scalar1=-1.0)
-        nc.vector.tensor_copy(out=sin_pm[:, :, 1, :], in_=rope_pairs[:, :, :, 1])
+        sin_pm = keep.tile([P, PARITIES, PAIRS, 2], F32, name="sin_pm")
 
-        for c in range(COMPONENTS):
-            for bank in range(BANKS_PER_COMPONENT):
-                col = bank * BANK_COLS
-                slab = slabs[c * SLABS_PER_COMPONENT + col // SLAB_COLS]
-                in_slab = col % SLAB_COLS
-                result = keep.tile([P, BANK_HEADS, PARITIES, D], F32, name="result%d_%d" % (c, bank))
+        def make_tables():
+            nc.scalar.copy(out=cos2[:], in_=rope_pairs[:, :, :, 0:1].to_broadcast([P, PARITIES, PAIRS, 2]))
+            nc.scalar.mul(sin_pm[:, :, :, 0], rope_pairs[:, :, :, 1], -1.0)
+            nc.scalar.copy(out=sin_pm[:, :, :, 1], in_=rope_pairs[:, :, :, 1])
+
+        grouped = []
+        x_codes = []
+        x_scales = []
+        for g in range(PASSES):
+            grouped.append(keep.tile([P, PARITIES * P * PACK], BF16, align_bytes=64, name="grouped%d" % g))
+            x_codes.append(keep.tile([P, PARITIES * P], U32, align_bytes=64, name="x_codes%d" % g))
+            x_scales.append(keep.tile([P, PARITIES * P], U8, align_bytes=64, name="x_scales%d" % g))
+
+        def turn_x(g, copy):
+            xt = psum.tile([P, PARITIES, 2, P], F32, tag="bank", name="xt")
+            for par in range(PARITIES):
+                x_words = x_sb[:, par, :].bitcast(F32)
+                for u in range(2):
+                    nc.tensor.transpose(xt[:, par, u, :], x_words[:, 256 * g + u : 256 * (g + 1) : 2], identity[:])
+            copy(
+                out=grouped[g][:].bitcast(F32).rearrange("p (par t u) -> p par t u", par=PARITIES, u=2),
+                in_=xt[:].rearrange("p par u t -> p par t u"),
+            )
+
+        def quantise_x(g):
+            nc.vector.quantize_mx(out=x_codes[g][:].bitcast(FP8X4), scales=x_scales[g][:], in_=grouped[g][:])
+
+        def multiply(acc, group, par, col, g):
+            nc.tensor.matmul_mx(
+                out=acc[:],
+                lhsT=x_codes[g][:, par * P : (par + 1) * P].bitcast(FP8X4),
+                lhsT_scale=x_scales[g][:, par * P : (par + 1) * P],
+                rhs=slabs[group][:, g, 2 * col : 2 * (col + BANK_COLS)].bitcast(FP4X4),
+                rhs_scale=planes[group][:, g, col : col + BANK_COLS],
+                start=(g == 0),
+                stop=(g == PASSES - 1),
+            )
+
+        def finish(acc, group, par, result):
+            by_head = acc[:].rearrange("p (h d) -> p h d", h=BANK_HEADS)
+            if group[0] == V:
+                nc.scalar.copy(out=result[:, :, par, :], in_=by_head)
+                return
+            straight = work.tile([P, BANK_HEADS, D], F32, name="straight")
+            nc.vector.tensor_tensor(
+                out=straight[:],
+                in0=by_head,
+                in1=cos2[:, par, :, :].rearrange("p j e -> p (j e)").unsqueeze(1).to_broadcast([P, BANK_HEADS, D]),
+                op=MULT,
+            )
+            crossed = work.tile([P, BANK_HEADS * PAIRS, 2], F32, name="crossed")
+            nc.vector.tensor_tensor(
+                out=crossed[:].rearrange("p (h j) e -> p h j e", h=BANK_HEADS),
+                in0=acc[:].rearrange("p (h j e) -> p h j e", h=BANK_HEADS, e=2)[:, :, :, ::-1],
+                in1=sin_pm[:, par, :, :].unsqueeze(1).to_broadcast([P, BANK_HEADS, PAIRS, 2]),
+                op=MULT,
+            )
+            nc.gpsimd.tensor_tensor(
+                out=result[:, :, par, :],
+                in0=straight[:],
+                in1=crossed[:].rearrange("p (h j) e -> p h (j e)", h=BANK_HEADS),
+                op=ADD,
+            )
+
+        def store(group, col, result):
+            head = (group[1] + col) // D
+            out = outs[group[0]]
+            for b in range(BATCH):
+                nc.sync.dma_start(
+                    out=out[b, head : head + BANK_HEADS, :, :].rearrange("h (m par) d -> m h (par d)", par=PARITIES),
+                    in_=result[b:P:BATCH, :, :, :].rearrange("p h par d -> p h (par d)"),
+                )
+
+        turn_x(0, nc.scalar.copy)
+        turn_x(1, nc.vector.tensor_copy)
+        quantise_x(0)
+        quantise_x(1)
+        nc.vector.memset(planes[v_last][:].bitcast(I32), 0)
+        load_scales(v_last)
+        load_words(v_last, every_pass, slice(0, HALF))
+
+        first_cols = range(0, HALF, BANK_COLS)
+        accs = {}
+        for col in first_cols:
+            for par in range(PARITIES):
+                accs[col, par] = psum.tile([P, BANK_COLS], F32, tag="bank", name="acc")
+        for g in range(PASSES):
+            for col in first_cols:
+                for par in range(PARITIES):
+                    multiply(accs[col, par], v_first, par, col, g)
+            if g == 0:
+                turn_x(2, nc.scalar.copy)
+                turn_x(3, nc.vector.tensor_copy)
+                quantise_x(2)
+                quantise_x(3)
+                make_tables()
+        for col in first_cols:
+            result = keep.tile([P, BANK_HEADS, PARITIES, D], F32, name="result%d_%d" % (V, col))
+            for par in range(PARITIES):
+                finish(accs[col, par], v_first, par, result)
+            store(v_first, col, result)
+
+        for group in groups[1:]:
+            for col in range(0, group[2], BANK_COLS):
+                result = keep.tile([P, BANK_HEADS, PARITIES, D], F32, name="result%d_%d" % (group[0], group[1] + col))
                 for par in range(PARITIES):
                     acc = psum.tile([P, BANK_COLS], F32, tag="bank", name="acc")
                     for g in range(PASSES):
-                        nc.tensor.matmul_mx(
-                            out=acc[:],
-                            lhsT=x_codes[par][:, g * P : (g + 1) * P].bitcast(FP8X4),
-                            lhsT_scale=x_scales[par][:, g * P : (g + 1) * P],
-                            rhs=slab[:, g, 2 * in_slab : 2 * (in_slab + BANK_COLS)].bitcast(FP4X4),
-                            rhs_scale=planes[c][:, g, col : col + BANK_COLS],
-                            start=(g == 0),
-                            stop=(g == PASSES - 1),
-                        )
-                    by_head = acc[:].rearrange("p (h d) -> p h d", h=BANK_HEADS)
-                    if c == COMPONENTS - 1:
-                        nc.scalar.copy(out=result[:, :, par, :], in_=by_head)
-                    else:
-                        by_pair = acc[:].rearrange("p (h j e) -> p h j e", h=BANK_HEADS, e=2)
-                        straight = work.tile([P, BANK_HEADS, D], F32, name="straight")
-                        nc.vector.tensor_tensor(
-                            out=straight[:],
-                            in0=by_head,
-                            in1=cos2[:, par, :, :].rearrange("p j e -> p (j e)").unsqueeze(1).to_broadcast([P, BANK_HEADS, D]),
-                            op=MULT,
-                        )
-                        crossed = work.tile([P, 2, BANK_HEADS, PAIRS], F32, name="crossed")
-                        for e in range(2):
-                            nc.vector.tensor_tensor(
-                                out=crossed[:, e, :, :],
-                                in0=by_pair[:, :, :, 1 - e],
-                                in1=sin_pm[:, par, e, :].unsqueeze(1).to_broadcast([P, BANK_HEADS, PAIRS]),
-                                op=MULT,
-                            )
-                        nc.gpsimd.tensor_tensor(
-                            out=result[:, :, par, :].rearrange("p h (j e) -> p h j e", e=2),
-                            in0=straight[:].rearrange("p h (j e) -> p h j e", e=2),
-                            in1=crossed[:].rearrange("p e h j -> p h j e"),
-                            op=ADD,
-                        )
-                for h in range(BANK_HEADS):
-                    head = bank * BANK_HEADS + h
-                    nc.sync.dma_start(
-                        out=outs[c][:, head, :, :].rearrange("b (m par) d -> m b (par d)", par=PARITIES),
-                        in_=result[:, h, :, :].rearrange("p par d -> p (par d)"),
-                    )
+                        multiply(acc, group, par, col, g)
+                    finish(acc, group, par, result)
+                store(group, col, result)

@@ -31,6 +31,7 @@ PASSES = HID // K_PASS
 BANK_COLS = 512
 BANK_HEADS = BANK_COLS // D
 HALF = COMPONENT_COLS // 2
+HALF_HEADS = HALF // D
 PARITIES = 2
 
 FLOPS = 2 * BATCH * POSITIONS * HID * COMPONENTS * COMPONENT_COLS
@@ -42,27 +43,33 @@ def tile_attention_pa_kernel(tc, x, rope, qkv_w_words, qkv_w_scales, out_0, out_
 
     with ExitStack() as ctx:
         keep = ctx.enter_context(tc.tile_pool(name="keep", bufs=1))
-        work = ctx.enter_context(tc.tile_pool(name="work", bufs=3))
+        work = ctx.enter_context(tc.tile_pool(name="work", bufs=4))
         psum = ctx.enter_context(tc.psum_pool(name="psum", bufs=8))
         ctx.enter_context(tc.manual_schedule())
 
-        v_first = (V, 0, HALF)
-        q_all = (Q, 0, COMPONENT_COLS)
-        k_all = (K, 0, COMPONENT_COLS)
-        v_last = (V, HALF, HALF)
-        groups = [v_first, q_all, k_all, v_last]
+        halves = [(Q, 0), (Q, HALF), (V, 0), (K, 0), (K, HALF), (V, HALF)]
 
-        planes = {}
+        first_plane = keep.tile([P, PASSES, HALF], U8, align_bytes=64, name="first_plane")
+        second_plane = keep.tile([P, PASSES, HALF], U8, align_bytes=64, name="second_plane")
+        k_plane = keep.tile([P, PASSES, COMPONENT_COLS], U8, align_bytes=64, name="k_plane")
+        v_plane = keep.tile([P, PASSES, COMPONENT_COLS], U8, align_bytes=64, name="v_plane")
+        plane_at = {
+            (Q, 0): (first_plane, 0),
+            (Q, HALF): (second_plane, 0),
+            (K, 0): (k_plane, 0),
+            (K, HALF): (k_plane, HALF),
+            (V, 0): (v_plane, 0),
+            (V, HALF): (v_plane, HALF),
+        }
         slabs = {}
-        for group in groups:
-            planes[group] = keep.tile([P, PASSES, group[2]], U8, align_bytes=64, name="plane%d_%d" % group[:2])
-            slabs[group] = keep.tile([P, PASSES, 2 * group[2]], U8, align_bytes=64, name="slab%d_%d" % group[:2])
+        for half in halves:
+            slabs[half] = keep.tile([P, PASSES, 2 * HALF], U8, align_bytes=64, name="slab%d_%d" % half)
 
         identity = keep.tile([P, P], F32, name="identity")
         make_identity(nc, identity[:])
-        nc.vector.memset(planes[v_first][:].bitcast(I32), 0)
-        nc.gpsimd.memset(planes[q_all][:].bitcast(I32), 0)
-        nc.vector.memset(planes[k_all][:].bitcast(I32), 0)
+        nc.vector.memset(first_plane[:].bitcast(I32), 0)
+        nc.gpsimd.memset(second_plane[:].bitcast(I32), 0)
+        nc.vector.memset(v_plane[:].bitcast(I32), 0)
 
         rope_sb = keep.tile([P, PARITIES, D], BF16, name="rope_sb")
         rope_rows = rope.rearrange("(m par) o d -> m par (o d)", par=PARITIES)
@@ -76,36 +83,31 @@ def tile_attention_pa_kernel(tc, x, rope, qkv_w_words, qkv_w_scales, out_0, out_
             for par in range(PARITIES):
                 nc.sync.dma_start(out=x_sb[:, par, ks], in_=x_by_parity[par][:, :, ks])
 
-        def load_scales(group):
-            c, first, width = group
-            cols = slice(c * COMPONENT_COLS + first, c * COMPONENT_COLS + first + width)
+        def load_scales(plane, first_col):
+            width = plane.shape[2]
             for r in range(4):
                 nc.sync.dma_start(
-                    out=planes[group][r:P:32, :, :].bitcast(I32),
-                    in_=qkv_w_scales[:, r:16:4, cols].rearrange("g q n -> q g n").bitcast(I32),
+                    out=plane[r:P:32, :, :].bitcast(I32),
+                    in_=qkv_w_scales[:, r:16:4, first_col : first_col + width].rearrange("g q n -> q g n").bitcast(I32),
                 )
 
-        def load_words(group, passes, cols):
-            c, first, width = group
-            base = 2 * (c * COMPONENT_COLS + first)
+        def load_words(half, passes):
+            base = 2 * (half[0] * COMPONENT_COLS + half[1])
             nc.sync.dma_start(
-                out=slabs[group][:, passes, 2 * cols.start : 2 * cols.stop].bitcast(I32),
-                in_=qkv_w_words[passes, :, base + 2 * cols.start : base + 2 * cols.stop]
-                .rearrange("g p n -> p g n")
-                .bitcast(I32),
+                out=slabs[half][:, passes, :].bitcast(I32),
+                in_=qkv_w_words[passes, :, base : base + 2 * HALF].rearrange("g p n -> p g n").bitcast(I32),
             )
 
         every_pass = slice(0, PASSES)
         load_x(slice(0, HID // 2))
-        load_scales(v_first)
-        load_words(v_first, slice(0, PASSES // 2), slice(0, HALF))
+        load_scales(first_plane, 0)
+        load_words((Q, 0), slice(0, PASSES // 2))
         load_x(slice(HID // 2, HID))
-        load_words(v_first, slice(PASSES // 2, PASSES), slice(0, HALF))
-        load_scales(q_all)
-        load_words(q_all, every_pass, slice(0, HALF))
-        load_words(q_all, every_pass, slice(HALF, COMPONENT_COLS))
-        load_scales(k_all)
-        load_words(k_all, every_pass, slice(0, COMPONENT_COLS))
+        load_words((Q, 0), slice(PASSES // 2, PASSES))
+        load_scales(second_plane, HALF)
+        load_words((Q, HALF), every_pass)
+        load_scales(v_plane, V * COMPONENT_COLS)
+        load_words((V, 0), every_pass)
 
         rope_pairs = rope_sb[:].rearrange("p par (j e) -> p par j e", e=2)
         cos2 = keep.tile([P, PARITIES, PAIRS, 2], F32, name="cos2")
@@ -138,87 +140,87 @@ def tile_attention_pa_kernel(tc, x, rope, qkv_w_words, qkv_w_scales, out_0, out_
         def quantise_x(g):
             nc.vector.quantize_mx(out=x_codes[g][:].bitcast(FP8X4), scales=x_scales[g][:], in_=grouped[g][:])
 
-        def multiply(acc, group, par, col, g):
+        def multiply(acc, half, par, col, g):
+            plane, start = plane_at[half]
             nc.tensor.matmul_mx(
                 out=acc[:],
                 lhsT=x_codes[g][:, par * P : (par + 1) * P].bitcast(FP8X4),
                 lhsT_scale=x_scales[g][:, par * P : (par + 1) * P],
-                rhs=slabs[group][:, g, 2 * col : 2 * (col + BANK_COLS)].bitcast(FP4X4),
-                rhs_scale=planes[group][:, g, col : col + BANK_COLS],
+                rhs=slabs[half][:, g, 2 * col : 2 * (col + BANK_COLS)].bitcast(FP4X4),
+                rhs_scale=plane[:, g, start + col : start + col + BANK_COLS],
                 start=(g == 0),
                 stop=(g == PASSES - 1),
             )
 
-        def finish(acc, group, par, result):
-            by_head = acc[:].rearrange("p (h d) -> p h d", h=BANK_HEADS)
-            if group[0] == V:
-                nc.scalar.copy(out=result[:, :, par, :], in_=by_head)
-                return
-            straight = work.tile([P, BANK_HEADS, D], F32, name="straight")
+        def rope_products(acc, par, straight, crossed):
             nc.vector.tensor_tensor(
-                out=straight[:],
-                in0=by_head,
+                out=straight,
+                in0=acc[:].rearrange("p (h d) -> p h d", h=BANK_HEADS),
                 in1=cos2[:, par, :, :].rearrange("p j e -> p (j e)").unsqueeze(1).to_broadcast([P, BANK_HEADS, D]),
                 op=MULT,
             )
-            crossed = work.tile([P, BANK_HEADS * PAIRS, 2], F32, name="crossed")
             nc.vector.tensor_tensor(
-                out=crossed[:].rearrange("p (h j) e -> p h j e", h=BANK_HEADS),
+                out=crossed.rearrange("p h (j e) -> p h j e", e=2),
                 in0=acc[:].rearrange("p (h j e) -> p h j e", h=BANK_HEADS, e=2)[:, :, :, ::-1],
                 in1=sin_pm[:, par, :, :].unsqueeze(1).to_broadcast([P, BANK_HEADS, PAIRS, 2]),
                 op=MULT,
             )
-            nc.gpsimd.tensor_tensor(
-                out=result[:, :, par, :],
-                in0=straight[:],
-                in1=crossed[:].rearrange("p (h j) e -> p h (j e)", h=BANK_HEADS),
-                op=ADD,
-            )
 
-        def store(group, col, result):
-            head = (group[1] + col) // D
-            out = outs[group[0]]
+        def store(half, first_head, heads, result):
+            head = half[1] // D + first_head
+            out = outs[half[0]]
             for b in range(BATCH):
                 nc.sync.dma_start(
-                    out=out[b, head : head + BANK_HEADS, :, :].rearrange("h (m par) d -> m h (par d)", par=PARITIES),
-                    in_=result[b:P:BATCH, :, :, :].rearrange("p h par d -> p h (par d)"),
+                    out=out[b, head : head + heads, :, :].rearrange("h (m par) d -> m h (par d)", par=PARITIES),
+                    in_=result[b:P:BATCH, first_head : first_head + heads, :, :].rearrange("p h par d -> p h (par d)"),
                 )
 
         turn_x(0, nc.scalar.copy)
         turn_x(1, nc.vector.tensor_copy)
         quantise_x(0)
         quantise_x(1)
-        nc.vector.memset(planes[v_last][:].bitcast(I32), 0)
-        load_scales(v_last)
-        load_words(v_last, every_pass, slice(0, HALF))
+        nc.vector.memset(k_plane[:].bitcast(I32), 0)
+        load_scales(k_plane, K * COMPONENT_COLS)
+        load_words((K, 0), every_pass)
+        load_words((K, HALF), every_pass)
+        load_words((V, HALF), every_pass)
 
-        first_cols = range(0, HALF, BANK_COLS)
-        accs = {}
-        for col in first_cols:
-            for par in range(PARITIES):
-                accs[col, par] = psum.tile([P, BANK_COLS], F32, tag="bank", name="acc")
-        for g in range(PASSES):
-            for col in first_cols:
+        for half in halves:
+            result = keep.tile([P, HALF_HEADS, PARITIES, D], F32, name="result%d_%d" % half)
+            accs = {}
+            for col in range(0, HALF, BANK_COLS):
                 for par in range(PARITIES):
-                    multiply(accs[col, par], v_first, par, col, g)
-            if g == 0:
-                turn_x(2, nc.scalar.copy)
-                turn_x(3, nc.vector.tensor_copy)
-                quantise_x(2)
-                quantise_x(3)
-                make_tables()
-        for col in first_cols:
-            result = keep.tile([P, BANK_HEADS, PARITIES, D], F32, name="result%d_%d" % (V, col))
-            for par in range(PARITIES):
-                finish(accs[col, par], v_first, par, result)
-            store(v_first, col, result)
-
-        for group in groups[1:]:
-            for col in range(0, group[2], BANK_COLS):
-                result = keep.tile([P, BANK_HEADS, PARITIES, D], F32, name="result%d_%d" % (group[0], group[1] + col))
+                    accs[col, par] = psum.tile([P, BANK_COLS], F32, tag="bank", name="acc")
+            if half == halves[0]:
+                for g in range(PASSES):
+                    for col, par in accs:
+                        multiply(accs[col, par], half, par, col, g)
+                    if g == 0:
+                        turn_x(2, nc.scalar.copy)
+                        turn_x(3, nc.vector.tensor_copy)
+                        quantise_x(2)
+                        quantise_x(3)
+                        make_tables()
+            for col in range(0, HALF, BANK_COLS):
+                first_head = col // D
+                target = result[:, first_head : first_head + BANK_HEADS, :, :]
+                if half[0] != V:
+                    straight = work.tile([P, PARITIES, BANK_HEADS, D], F32, name="straight")
+                    crossed = work.tile([P, PARITIES, BANK_HEADS, D], F32, name="crossed")
                 for par in range(PARITIES):
-                    acc = psum.tile([P, BANK_COLS], F32, tag="bank", name="acc")
-                    for g in range(PASSES):
-                        multiply(acc, group, par, col, g)
-                    finish(acc, group, par, result)
-                store(group, col, result)
+                    acc = accs[col, par]
+                    if half != halves[0]:
+                        for g in range(PASSES):
+                            multiply(acc, half, par, col, g)
+                    if half[0] == V:
+                        nc.scalar.copy(out=target[:, :, par, :], in_=acc[:].rearrange("p (h d) -> p h d", h=BANK_HEADS))
+                    else:
+                        rope_products(acc, par, straight[:, par, :, :], crossed[:, par, :, :])
+                if half[0] != V:
+                    nc.gpsimd.tensor_tensor(
+                        out=target.rearrange("p h par d -> p par h d"), in0=straight[:], in1=crossed[:], op=ADD
+                    )
+                if half == halves[-1]:
+                    store(half, first_head, BANK_HEADS, result)
+            if half != halves[-1]:
+                store(half, 0, HALF_HEADS, result)

@@ -74,7 +74,7 @@ def tile_attention_pa_kernel(tc, x, rope, qkv_w_words, qkv_w_scales, out_0, out_
         rope_sb = keep.tile([P, PARITIES, D], BF16, name="rope_sb")
         rope_rows = rope.rearrange("(m par) o d -> m par (o d)", par=PARITIES)
         for b in range(BATCH):
-            nc.gpsimd.dma_start(out=rope_sb[b:P:BATCH, :, :], in_=rope_rows)
+            nc.scalar.dma_start(out=rope_sb[b:P:BATCH, :, :], in_=rope_rows)
 
         x_by_parity = x.rearrange("b (m par) k -> par m b k", par=PARITIES)
         x_sb = keep.tile([P, PARITIES, HID], BF16, name="x_sb")
@@ -91,23 +91,22 @@ def tile_attention_pa_kernel(tc, x, rope, qkv_w_words, qkv_w_scales, out_0, out_
                     in_=qkv_w_scales[:, r:16:4, first_col : first_col + width].rearrange("g q n -> q g n").bitcast(I32),
                 )
 
-        def load_words(half, passes):
+        def load_words(half, first, last):
             base = 2 * (half[0] * COMPONENT_COLS + half[1])
             nc.sync.dma_start(
-                out=slabs[half][:, passes, :].bitcast(I32),
-                in_=qkv_w_words[passes, :, base : base + 2 * HALF].rearrange("g p n -> p g n").bitcast(I32),
+                out=slabs[half][:, :, 2 * first : 2 * last].bitcast(I32),
+                in_=qkv_w_words[:, :, base + 2 * first : base + 2 * last].rearrange("g p n -> p g n").bitcast(I32),
             )
 
-        every_pass = slice(0, PASSES)
         load_x(slice(0, HID // 2))
-        load_scales(first_plane, 0)
-        load_words((Q, 0), slice(0, PASSES // 2))
         load_x(slice(HID // 2, HID))
-        load_words((Q, 0), slice(PASSES // 2, PASSES))
+        load_scales(first_plane, 0)
+        load_words((Q, 0), 0, BANK_COLS)
+        load_words((Q, 0), BANK_COLS, HALF)
         load_scales(second_plane, HALF)
-        load_words((Q, HALF), every_pass)
+        load_words((Q, HALF), 0, HALF)
         load_scales(v_plane, V * COMPONENT_COLS)
-        load_words((V, 0), every_pass)
+        load_words((V, 0), 0, HALF)
 
         rope_pairs = rope_sb[:].rearrange("p par (j e) -> p par j e", e=2)
         cos2 = keep.tile([P, PARITIES, PAIRS, 2], F32, name="cos2")
@@ -175,32 +174,21 @@ def tile_attention_pa_kernel(tc, x, rope, qkv_w_words, qkv_w_scales, out_0, out_
                     in_=result[b:P:BATCH, first_head : first_head + heads, :, :].rearrange("p h par d -> p h (par d)"),
                 )
 
-        turn_x(0, nc.scalar.copy)
-        turn_x(1, nc.vector.tensor_copy)
-        quantise_x(0)
-        quantise_x(1)
+        for g in range(PASSES):
+            turn_x(g, nc.vector.tensor_copy if g % 2 else nc.scalar.copy)
+            if g % 2:
+                quantise_x(g - 1)
+                quantise_x(g)
+        make_tables()
         nc.vector.memset(k_plane[:].bitcast(I32), 0)
         load_scales(k_plane, K * COMPONENT_COLS)
-        load_words((K, 0), every_pass)
-        load_words((K, HALF), every_pass)
-        load_words((V, HALF), every_pass)
+        load_words((K, 0), 0, HALF)
+        load_words((K, HALF), 0, HALF)
+        load_words((V, HALF), 0, HALF)
 
+        waiting = []
         for half in halves:
             result = keep.tile([P, HALF_HEADS, PARITIES, D], F32, name="result%d_%d" % half)
-            accs = {}
-            for col in range(0, HALF, BANK_COLS):
-                for par in range(PARITIES):
-                    accs[col, par] = psum.tile([P, BANK_COLS], F32, tag="bank", name="acc")
-            if half == halves[0]:
-                for g in range(PASSES):
-                    for col, par in accs:
-                        multiply(accs[col, par], half, par, col, g)
-                    if g == 0:
-                        turn_x(2, nc.scalar.copy)
-                        turn_x(3, nc.vector.tensor_copy)
-                        quantise_x(2)
-                        quantise_x(3)
-                        make_tables()
             for col in range(0, HALF, BANK_COLS):
                 first_head = col // D
                 target = result[:, first_head : first_head + BANK_HEADS, :, :]
@@ -208,10 +196,9 @@ def tile_attention_pa_kernel(tc, x, rope, qkv_w_words, qkv_w_scales, out_0, out_
                     straight = work.tile([P, PARITIES, BANK_HEADS, D], F32, name="straight")
                     crossed = work.tile([P, PARITIES, BANK_HEADS, D], F32, name="crossed")
                 for par in range(PARITIES):
-                    acc = accs[col, par]
-                    if half != halves[0]:
-                        for g in range(PASSES):
-                            multiply(acc, half, par, col, g)
+                    acc = psum.tile([P, BANK_COLS], F32, tag="bank", name="acc")
+                    for g in range(PASSES):
+                        multiply(acc, half, par, col, g)
                     if half[0] == V:
                         nc.scalar.copy(out=target[:, :, par, :], in_=acc[:].rearrange("p (h d) -> p h d", h=BANK_HEADS))
                     else:
@@ -220,7 +207,11 @@ def tile_attention_pa_kernel(tc, x, rope, qkv_w_words, qkv_w_scales, out_0, out_
                     nc.gpsimd.tensor_tensor(
                         out=target.rearrange("p h par d -> p par h d"), in0=straight[:], in1=crossed[:], op=ADD
                     )
-                if half == halves[-1]:
-                    store(half, first_head, BANK_HEADS, result)
-            if half != halves[-1]:
+                if half in halves[-2:]:
+                    for late in waiting:
+                        store(*late)
+                    waiting = [(half, first_head, BANK_HEADS, result)]
+            if half not in halves[-2:]:
                 store(half, 0, HALF_HEADS, result)
+        for late in waiting:
+            store(*late)

@@ -47,29 +47,18 @@ def tile_attention_pa_kernel(tc, x, rope, qkv_w_words, qkv_w_scales, out_0, out_
         psum = ctx.enter_context(tc.psum_pool(name="psum", bufs=8))
         ctx.enter_context(tc.manual_schedule())
 
-        halves = [(Q, 0), (Q, HALF), (V, 0), (K, 0), (K, HALF), (V, HALF)]
+        halves = [(c, first) for c in (Q, K, V) for first in (0, HALF)]
 
-        first_plane = keep.tile([P, PASSES, HALF], U8, align_bytes=64, name="first_plane")
-        second_plane = keep.tile([P, PASSES, HALF], U8, align_bytes=64, name="second_plane")
-        k_plane = keep.tile([P, PASSES, COMPONENT_COLS], U8, align_bytes=64, name="k_plane")
-        v_plane = keep.tile([P, PASSES, COMPONENT_COLS], U8, align_bytes=64, name="v_plane")
-        plane_at = {
-            (Q, 0): (first_plane, 0),
-            (Q, HALF): (second_plane, 0),
-            (K, 0): (k_plane, 0),
-            (K, HALF): (k_plane, HALF),
-            (V, 0): (v_plane, 0),
-            (V, HALF): (v_plane, HALF),
-        }
-        slabs = {}
-        for half in halves:
-            slabs[half] = keep.tile([P, PASSES, 2 * HALF], U8, align_bytes=64, name="slab%d_%d" % half)
+        planes = []
+        slabs = []
+        for c in range(COMPONENTS):
+            planes.append(keep.tile([P, PASSES, COMPONENT_COLS], U8, align_bytes=64, name="plane%d" % c))
+            slabs.append(keep.tile([P, PASSES, 2 * COMPONENT_COLS], U8, align_bytes=64, name="slab%d" % c))
 
         identity = keep.tile([P, P], F32, name="identity")
         make_identity(nc, identity[:])
-        nc.vector.memset(first_plane[:].bitcast(I32), 0)
-        nc.gpsimd.memset(second_plane[:].bitcast(I32), 0)
-        nc.vector.memset(v_plane[:].bitcast(I32), 0)
+        nc.vector.memset(planes[Q][:].bitcast(I32), 0)
+        nc.gpsimd.memset(planes[K][:].bitcast(I32), 0)
 
         rope_sb = keep.tile([P, PARITIES, D], BF16, name="rope_sb")
         rope_rows = rope.rearrange("(m par) o d -> m par (o d)", par=PARITIES)
@@ -79,34 +68,24 @@ def tile_attention_pa_kernel(tc, x, rope, qkv_w_words, qkv_w_scales, out_0, out_
         x_by_parity = x.rearrange("b (m par) k -> par m b k", par=PARITIES)
         x_sb = keep.tile([P, PARITIES, HID], BF16, name="x_sb")
 
-        def load_x(ks):
-            for par in range(PARITIES):
-                nc.sync.dma_start(out=x_sb[:, par, ks], in_=x_by_parity[par][:, :, ks])
+        for par in range(PARITIES):
+            nc.sync.dma_start(out=x_sb[:, par, :], in_=x_by_parity[par])
 
-        def load_scales(plane, first_col):
-            width = plane.shape[2]
+        def load_weights(c):
+            cols = slice(c * COMPONENT_COLS, (c + 1) * COMPONENT_COLS)
             for r in range(4):
                 nc.sync.dma_start(
-                    out=plane[r:P:32, :, :].bitcast(I32),
-                    in_=qkv_w_scales[:, r:16:4, first_col : first_col + width].rearrange("g q n -> q g n").bitcast(I32),
+                    out=planes[c][r:P:32, :, :].bitcast(I32),
+                    in_=qkv_w_scales[:, r:16:4, cols].rearrange("g q n -> q g n").bitcast(I32),
+                )
+            for g in range(0, PASSES, 2):
+                nc.sync.dma_start(
+                    out=slabs[c][:, g : g + 2, :].bitcast(I32),
+                    in_=qkv_w_words[g : g + 2, :, 2 * cols.start : 2 * cols.stop].rearrange("g p n -> p g n").bitcast(I32),
                 )
 
-        def load_words(half, first, last):
-            base = 2 * (half[0] * COMPONENT_COLS + half[1])
-            nc.sync.dma_start(
-                out=slabs[half][:, :, 2 * first : 2 * last].bitcast(I32),
-                in_=qkv_w_words[:, :, base + 2 * first : base + 2 * last].rearrange("g p n -> p g n").bitcast(I32),
-            )
-
-        load_x(slice(0, HID // 2))
-        load_x(slice(HID // 2, HID))
-        load_scales(first_plane, 0)
-        load_words((Q, 0), 0, BANK_COLS)
-        load_words((Q, 0), BANK_COLS, HALF)
-        load_scales(second_plane, HALF)
-        load_words((Q, HALF), 0, HALF)
-        load_scales(v_plane, V * COMPONENT_COLS)
-        load_words((V, 0), 0, HALF)
+        load_weights(Q)
+        load_weights(K)
 
         rope_pairs = rope_sb[:].rearrange("p par (j e) -> p par j e", e=2)
         cos2 = keep.tile([P, PARITIES, PAIRS, 2], F32, name="cos2")
@@ -139,14 +118,13 @@ def tile_attention_pa_kernel(tc, x, rope, qkv_w_words, qkv_w_scales, out_0, out_
         def quantise_x(g):
             nc.vector.quantize_mx(out=x_codes[g][:].bitcast(FP8X4), scales=x_scales[g][:], in_=grouped[g][:])
 
-        def multiply(acc, half, par, col, g):
-            plane, start = plane_at[half]
+        def multiply(acc, c, par, col, g):
             nc.tensor.matmul_mx(
                 out=acc[:],
                 lhsT=x_codes[g][:, par * P : (par + 1) * P].bitcast(FP8X4),
                 lhsT_scale=x_scales[g][:, par * P : (par + 1) * P],
-                rhs=slabs[half][:, g, 2 * col : 2 * (col + BANK_COLS)].bitcast(FP4X4),
-                rhs_scale=plane[:, g, start + col : start + col + BANK_COLS],
+                rhs=slabs[c][:, g, 2 * col : 2 * (col + BANK_COLS)].bitcast(FP4X4),
+                rhs_scale=planes[c][:, g, col : col + BANK_COLS],
                 start=(g == 0),
                 stop=(g == PASSES - 1),
             )
@@ -180,11 +158,8 @@ def tile_attention_pa_kernel(tc, x, rope, qkv_w_words, qkv_w_scales, out_0, out_
                 quantise_x(g - 1)
                 quantise_x(g)
         make_tables()
-        nc.vector.memset(k_plane[:].bitcast(I32), 0)
-        load_scales(k_plane, K * COMPONENT_COLS)
-        load_words((K, 0), 0, HALF)
-        load_words((K, HALF), 0, HALF)
-        load_words((V, HALF), 0, HALF)
+        nc.vector.memset(planes[V][:].bitcast(I32), 0)
+        load_weights(V)
 
         waiting = []
         for half in halves:
@@ -198,7 +173,7 @@ def tile_attention_pa_kernel(tc, x, rope, qkv_w_words, qkv_w_scales, out_0, out_
                 for par in range(PARITIES):
                     acc = psum.tile([P, BANK_COLS], F32, tag="bank", name="acc")
                     for g in range(PASSES):
-                        multiply(acc, half, par, col, g)
+                        multiply(acc, half[0], par, half[1] + col, g)
                     if half[0] == V:
                         nc.scalar.copy(out=target[:, :, par, :], in_=acc[:].rearrange("p (h d) -> p h d", h=BANK_HEADS))
                     else:
@@ -207,11 +182,11 @@ def tile_attention_pa_kernel(tc, x, rope, qkv_w_words, qkv_w_scales, out_0, out_
                     nc.gpsimd.tensor_tensor(
                         out=target.rearrange("p h par d -> p par h d"), in0=straight[:], in1=crossed[:], op=ADD
                     )
-                if half in halves[-2:]:
+                if half in halves[-3:]:
                     for late in waiting:
                         store(*late)
                     waiting = [(half, first_head, BANK_HEADS, result)]
-            if half not in halves[-2:]:
+            if half not in halves[-3:]:
                 store(half, 0, HALF_HEADS, result)
         for late in waiting:
             store(*late)

@@ -49,16 +49,23 @@ def tile_attention_pa_kernel(tc, x, rope, qkv_w_words, qkv_w_scales, out_0, out_
 
         halves = [(c, first) for c in (Q, K, V) for first in (0, HALF)]
 
-        planes = []
-        slabs = []
-        for c in range(COMPONENTS):
-            planes.append(keep.tile([P, PASSES, COMPONENT_COLS], U8, align_bytes=64, name="plane%d" % c))
-            slabs.append(keep.tile([P, PASSES, 2 * COMPONENT_COLS], U8, align_bytes=64, name="slab%d" % c))
+        q_planes = []
+        q_slabs = []
+        for h in range(2):
+            q_planes.append(keep.tile([P, PASSES, HALF], U8, align_bytes=64, name="q_plane%d" % h))
+            q_slabs.append(keep.tile([P, PASSES, 2 * HALF], U8, align_bytes=64, name="q_slab%d" % h))
+        planes = {}
+        slabs = {}
+        for c in (K, V):
+            planes[c] = keep.tile([P, PASSES, COMPONENT_COLS], U8, align_bytes=64, name="plane%d" % c)
+            slabs[c] = keep.tile([P, PASSES, 2 * COMPONENT_COLS], U8, align_bytes=64, name="slab%d" % c)
 
         identity = keep.tile([P, P], F32, name="identity")
         make_identity(nc, identity[:])
-        nc.vector.memset(planes[Q][:].bitcast(I32), 0)
+        nc.vector.memset(q_planes[0][:].bitcast(I32), 0)
+        nc.vector.memset(q_planes[1][:].bitcast(I32), 0)
         nc.gpsimd.memset(planes[K][:].bitcast(I32), 0)
+        nc.gpsimd.memset(planes[V][:].bitcast(I32), 0)
 
         rope_sb = keep.tile([P, PARITIES, D], BF16, name="rope_sb")
         rope_rows = rope.rearrange("(m par) o d -> m par (o d)", par=PARITIES)
@@ -71,21 +78,30 @@ def tile_attention_pa_kernel(tc, x, rope, qkv_w_words, qkv_w_scales, out_0, out_
         for par in range(PARITIES):
             nc.sync.dma_start(out=x_sb[:, par, :], in_=x_by_parity[par])
 
-        def load_weights(c):
-            cols = slice(c * COMPONENT_COLS, (c + 1) * COMPONENT_COLS)
+        def load_scales(plane, first_col):
+            width = plane.shape[2]
             for r in range(4):
                 nc.sync.dma_start(
-                    out=planes[c][r:P:32, :, :].bitcast(I32),
-                    in_=qkv_w_scales[:, r:16:4, cols].rearrange("g q n -> q g n").bitcast(I32),
-                )
-            for g in range(0, PASSES, 2):
-                nc.sync.dma_start(
-                    out=slabs[c][:, g : g + 2, :].bitcast(I32),
-                    in_=qkv_w_words[g : g + 2, :, 2 * cols.start : 2 * cols.stop].rearrange("g p n -> p g n").bitcast(I32),
+                    out=plane[r:P:32, :, :].bitcast(I32),
+                    in_=qkv_w_scales[:, r:16:4, first_col : first_col + width].rearrange("g q n -> q g n").bitcast(I32),
                 )
 
-        load_weights(Q)
-        load_weights(K)
+        def load_words(slab, first_col, passes):
+            width = slab.shape[2]
+            nc.sync.dma_start(
+                out=slab[:, passes, :].bitcast(I32),
+                in_=qkv_w_words[passes, :, 2 * first_col : 2 * first_col + width].rearrange("g p n -> p g n").bitcast(I32),
+            )
+
+        def load_component(c):
+            load_scales(planes[c], c * COMPONENT_COLS)
+            for g in range(0, PASSES, 2):
+                load_words(slabs[c], c * COMPONENT_COLS, slice(g, g + 2))
+
+        for h in range(2):
+            load_scales(q_planes[h], h * HALF)
+            load_words(q_slabs[h], h * HALF, slice(0, PASSES))
+        load_component(K)
 
         rope_pairs = rope_sb[:].rearrange("p par (j e) -> p par j e", e=2)
         cos2 = keep.tile([P, PARITIES, PAIRS, 2], F32, name="cos2")
@@ -118,13 +134,18 @@ def tile_attention_pa_kernel(tc, x, rope, qkv_w_words, qkv_w_scales, out_0, out_
         def quantise_x(g):
             nc.vector.quantize_mx(out=x_codes[g][:].bitcast(FP8X4), scales=x_scales[g][:], in_=grouped[g][:])
 
-        def multiply(acc, c, par, col, g):
+        def multiply(acc, half, par, col, width, g):
+            c, first = half
+            if c == Q:
+                plane, slab, start = q_planes[first // HALF], q_slabs[first // HALF], col
+            else:
+                plane, slab, start = planes[c], slabs[c], first + col
             nc.tensor.matmul_mx(
-                out=acc[:],
+                out=acc,
                 lhsT=x_codes[g][:, par * P : (par + 1) * P].bitcast(FP8X4),
                 lhsT_scale=x_scales[g][:, par * P : (par + 1) * P],
-                rhs=slabs[c][:, g, 2 * col : 2 * (col + BANK_COLS)].bitcast(FP4X4),
-                rhs_scale=planes[c][:, g, col : col + BANK_COLS],
+                rhs=slab[:, g, 2 * start : 2 * (start + width)].bitcast(FP4X4),
+                rhs_scale=plane[:, g, start : start + width],
                 start=(g == 0),
                 stop=(g == PASSES - 1),
             )
@@ -158,22 +179,40 @@ def tile_attention_pa_kernel(tc, x, rope, qkv_w_words, qkv_w_scales, out_0, out_
                 quantise_x(g - 1)
                 quantise_x(g)
         make_tables()
-        nc.vector.memset(planes[V][:].bitcast(I32), 0)
-        load_weights(V)
+        load_component(V)
+
+        def store_head(c, head, result):
+            nc.sync.dma_start(
+                out=outs[c][:, head, :, :].rearrange("b (m par) d -> m b (par d)", par=PARITIES),
+                in_=result.rearrange("p par d -> p (par d)"),
+            )
 
         waiting = []
         for half in halves:
             result = keep.tile([P, HALF_HEADS, PARITIES, D], F32, name="result%d_%d" % half)
+            accs = {}
+            if half == (K, 0):
+                for col in range(0, HALF, BANK_COLS):
+                    for par in range(PARITIES):
+                        accs[col, par] = psum.tile([P, BANK_COLS], F32, tag="bank", name="acc")
+                        for g in range(PASSES // 2):
+                            multiply(accs[col, par][:], half, par, col, BANK_COLS, g)
             for col in range(0, HALF, BANK_COLS):
                 first_head = col // D
                 target = result[:, first_head : first_head + BANK_HEADS, :, :]
+                if half == halves[-1] and col + BANK_COLS == HALF:
+                    break
                 if half[0] != V:
                     straight = work.tile([P, PARITIES, BANK_HEADS, D], F32, name="straight")
                     crossed = work.tile([P, PARITIES, BANK_HEADS, D], F32, name="crossed")
                 for par in range(PARITIES):
-                    acc = psum.tile([P, BANK_COLS], F32, tag="bank", name="acc")
-                    for g in range(PASSES):
-                        multiply(acc, half[0], par, half[1] + col, g)
+                    acc = accs.get((col, par))
+                    first_pass = PASSES // 2
+                    if acc is None:
+                        acc = psum.tile([P, BANK_COLS], F32, tag="bank", name="acc")
+                        first_pass = 0
+                    for g in range(first_pass, PASSES):
+                        multiply(acc[:], half, par, col, BANK_COLS, g)
                     if half[0] == V:
                         nc.scalar.copy(out=target[:, :, par, :], in_=acc[:].rearrange("p (h d) -> p h d", h=BANK_HEADS))
                     else:
@@ -190,3 +229,12 @@ def tile_attention_pa_kernel(tc, x, rope, qkv_w_words, qkv_w_scales, out_0, out_
                 store(half, 0, HALF_HEADS, result)
         for late in waiting:
             store(*late)
+        for h in range(BANK_HEADS):
+            acc = psum.tile([P, PARITIES, D], F32, tag="bank", name="acc")
+            for par in range(PARITIES):
+                for g in range(PASSES):
+                    multiply(acc[:, par, :], halves[-1], par, HALF - BANK_COLS + h * D, D, g)
+            copy = nc.vector.tensor_copy if h % 2 else nc.scalar.copy
+            head_result = result[:, HALF_HEADS - BANK_HEADS + h, :, :]
+            copy(out=head_result, in_=acc[:])
+            store_head(V, HEADS - BANK_HEADS + h, head_result)

@@ -68,9 +68,11 @@ def tile_attention_pa_kernel(tc, x, rope, qkv_w_words, qkv_w_scales, out_0, out_
         nc.gpsimd.memset(planes[V][:].bitcast(I32), 0)
 
         rope_sb = keep.tile([P, PARITIES, D], BF16, name="rope_sb")
-        rope_rows = rope.rearrange("(m par) o d -> m par (o d)", par=PARITIES)
-        for b in range(BATCH):
-            nc.scalar.dma_start(out=rope_sb[b:P:BATCH, :, :], in_=rope_rows)
+        rope_rows = rope.rearrange("(m par) o d -> m (par o d)", par=PARITIES)
+        nc.scalar.dma_start(
+            out=rope_sb[:].rearrange("p par d -> p (par d)"),
+            in_=rope_rows.unsqueeze(1).to_broadcast([POSITIONS // PARITIES, BATCH, PARITIES * D]),
+        )
 
         x_by_parity = x.rearrange("b (m par) k -> par m b k", par=PARITIES)
         x_sb = keep.tile([P, PARITIES, HID], BF16, name="x_sb")
@@ -164,11 +166,14 @@ def tile_attention_pa_kernel(tc, x, rope, qkv_w_words, qkv_w_scales, out_0, out_
                 op=MULT,
             )
 
+        two_queue_halves = [(K, 0), (V, 0), (V, HALF)]
+
         def store(half, first_head, heads, result):
             head = half[1] // D + first_head
             out = outs[half[0]]
-            for b in range(BATCH):
-                nc.sync.dma_start(
+            second = nc.scalar.dma_start if half in two_queue_halves else nc.sync.dma_start
+            for b, start_dma in enumerate((nc.sync.dma_start, second)):
+                start_dma(
                     out=out[b, head : head + heads, :, :].rearrange("h (m par) d -> m h (par d)", par=PARITIES),
                     in_=result[b:P:BATCH, first_head : first_head + heads, :, :].rearrange("p h par d -> p h (par d)"),
                 )
@@ -218,7 +223,9 @@ def tile_attention_pa_kernel(tc, x, rope, qkv_w_words, qkv_w_scales, out_0, out_
                     else:
                         rope_products(acc, par, straight[:, par, :, :], crossed[:, par, :, :])
                 if half[0] != V:
-                    nc.gpsimd.tensor_tensor(
+                    last_products = half == (K, HALF) and col + BANK_COLS == HALF
+                    add = nc.vector.tensor_tensor if last_products else nc.gpsimd.tensor_tensor
+                    add(
                         out=target.rearrange("p h par d -> p par h d"), in0=straight[:], in1=crossed[:], op=ADD
                     )
                 if half in halves[-3:]:

@@ -96,13 +96,15 @@ def tile_attention_pa_kernel(tc, x, rope, qkv_w_words, qkv_w_scales, out_0, out_
             )
 
         def load_component(c):
-            load_scales(planes[c], c * COMPONENT_COLS)
             for g in range(0, PASSES, 2):
                 load_words(slabs[c], c * COMPONENT_COLS, slice(g, g + 2))
 
         for h in range(2):
             load_scales(q_planes[h], h * HALF)
+        for h in range(2):
             load_words(q_slabs[h], h * HALF, slice(0, PASSES))
+        for c in (K, V):
+            load_scales(planes[c], c * COMPONENT_COLS)
         load_component(K)
 
         rope_pairs = rope_sb[:].rearrange("p par (j e) -> p par j e", e=2)

@@ -80,12 +80,12 @@ def tile_attention_pa_kernel(tc, x, rope, qkv_w_words, qkv_w_scales, out_0, out_
         for par in range(PARITIES):
             nc.sync.dma_start(out=x_sb[:, par, :], in_=x_by_parity[par])
 
-        def load_scales(plane, first_col):
+        def load_scales(plane, first_col, passes):
             width = plane.shape[2]
             for r in range(4):
                 nc.sync.dma_start(
-                    out=plane[r:P:32, :, :].bitcast(I32),
-                    in_=qkv_w_scales[:, r:16:4, first_col : first_col + width].rearrange("g q n -> q g n").bitcast(I32),
+                    out=plane[r:P:32, passes, :].bitcast(I32),
+                    in_=qkv_w_scales[passes, r:16:4, first_col : first_col + width].rearrange("g q n -> q g n").bitcast(I32),
                 )
 
         def load_words(slab, first_col, passes):
@@ -100,11 +100,12 @@ def tile_attention_pa_kernel(tc, x, rope, qkv_w_words, qkv_w_scales, out_0, out_
                 load_words(slabs[c], c * COMPONENT_COLS, slice(g, g + 2))
 
         for h in range(2):
-            load_scales(q_planes[h], h * HALF)
+            load_scales(q_planes[h], h * HALF, slice(0, PASSES))
         for h in range(2):
             load_words(q_slabs[h], h * HALF, slice(0, PASSES))
         for c in (K, V):
-            load_scales(planes[c], c * COMPONENT_COLS)
+            for g in range(0, PASSES, 2):
+                load_scales(planes[c], c * COMPONENT_COLS, slice(g, g + 2))
         load_component(K)
 
         rope_pairs = rope_sb[:].rearrange("p par (j e) -> p par j e", e=2)

@@ -169,13 +169,11 @@ def tile_attention_pa_kernel(tc, x, rope, qkv_w_words, qkv_w_scales, out_0, out_
                 op=MULT,
             )
 
-        two_queue_halves = [(K, 0), (V, 0), (V, HALF)]
-
         def store(half, first_head, heads, result):
             head = half[1] // D + first_head
             out = outs[half[0]]
-            second = nc.scalar.dma_start if half in two_queue_halves else nc.sync.dma_start
-            for b, start_dma in enumerate((nc.sync.dma_start, second)):
+            start_dma = nc.scalar.dma_start if half[0] == V else nc.sync.dma_start
+            for b in range(BATCH):
                 start_dma(
                     out=out[b, head : head + heads, :, :].rearrange("h (m par) d -> m h (par d)", par=PARITIES),
                     in_=result[b:P:BATCH, first_head : first_head + heads, :, :].rearrange("p h par d -> p h (par d)"),
@@ -195,7 +193,6 @@ def tile_attention_pa_kernel(tc, x, rope, qkv_w_words, qkv_w_scales, out_0, out_
                 in_=result.rearrange("p par d -> p (par d)"),
             )
 
-        waiting = []
         for half in halves:
             result = keep.tile([P, HALF_HEADS, PARITIES, D], F32, name="result%d_%d" % half)
             accs = {}
@@ -211,8 +208,8 @@ def tile_attention_pa_kernel(tc, x, rope, qkv_w_words, qkv_w_scales, out_0, out_
                 if half == halves[-1] and col + BANK_COLS == HALF:
                     break
                 if half[0] != V:
-                    straight = work.tile([P, PARITIES, BANK_HEADS, D], F32, name="straight")
-                    crossed = work.tile([P, PARITIES, BANK_HEADS, D], F32, name="crossed")
+                    straight = work.tile([P, BANK_HEADS, PARITIES, D], F32, name="straight")
+                    crossed = work.tile([P, BANK_HEADS, PARITIES, D], F32, name="crossed")
                 for par in range(PARITIES):
                     acc = accs.get((col, par))
                     first_pass = PASSES // 2
@@ -224,21 +221,20 @@ def tile_attention_pa_kernel(tc, x, rope, qkv_w_words, qkv_w_scales, out_0, out_
                     if half[0] == V:
                         nc.scalar.copy(out=target[:, :, par, :], in_=acc[:].rearrange("p (h d) -> p h d", h=BANK_HEADS))
                     else:
-                        rope_products(acc, par, straight[:, par, :, :], crossed[:, par, :, :])
+                        rope_products(acc, par, straight[:, :, par, :], crossed[:, :, par, :])
                 if half[0] != V:
                     last_products = half == (K, HALF) and col + BANK_COLS == HALF
                     add = nc.vector.tensor_tensor if last_products else nc.gpsimd.tensor_tensor
                     add(
-                        out=target.rearrange("p h par d -> p par h d"), in0=straight[:], in1=crossed[:], op=ADD
+                        out=target.rearrange("p h par d -> p (h par d)"),
+                        in0=straight[:].rearrange("p h par d -> p (h par d)"),
+                        in1=crossed[:].rearrange("p h par d -> p (h par d)"),
+                        op=ADD,
                     )
-                if half in halves[-3:]:
-                    for late in waiting:
-                        store(*late)
-                    waiting = [(half, first_head, BANK_HEADS, result)]
-            if half not in halves[-3:]:
+                if half[0] != Q:
+                    store(half, first_head, BANK_HEADS, result)
+            if half[0] == Q:
                 store(half, 0, HALF_HEADS, result)
-        for late in waiting:
-            store(*late)
         for h in range(BANK_HEADS):
             acc = psum.tile([P, PARITIES, D], F32, tag="bank", name="acc")
             for par in range(PARITIES):

from contextlib import ExitStack

import concourse.mybir as mybir
from concourse.masks import make_identity

F32 = mybir.dt.float32
BF16 = mybir.dt.bfloat16
I32 = mybir.dt.int32
U32 = mybir.dt.uint32
U8 = mybir.dt.uint8
FP8X4 = mybir.dt.float8_e4m3fn_x4
FP4X4 = mybir.dt.float4_e2m1fn_x4
MULT = mybir.AluOpType.mult
ADD = mybir.AluOpType.add

P = 128
BATCH = 2
POSITIONS = 128
HID = 2048
HEADS = 16
D = 128
PAIRS = D // 2
COMPONENTS = 3
Q, K, V = range(COMPONENTS)
COMPONENT_COLS = HEADS * D

PACK = 4
K_PASS = P * PACK
PASSES = HID // K_PASS

BANK_COLS = 512
BANK_HEADS = BANK_COLS // D
HALF = COMPONENT_COLS // 2
HALF_HEADS = HALF // D
PARITIES = 2

FLOPS = 2 * BATCH * POSITIONS * HID * COMPONENTS * COMPONENT_COLS


def tile_attention_pa_kernel(tc, x, rope, qkv_w_words, qkv_w_scales, out_0, out_1, out_2):
    nc = tc.nc
    outs = [out_0, out_1, out_2]

    with ExitStack() as ctx:
        keep = ctx.enter_context(tc.tile_pool(name="keep", bufs=1))
        work = ctx.enter_context(tc.tile_pool(name="work", bufs=4))
        psum = ctx.enter_context(tc.psum_pool(name="psum", bufs=8))
        ctx.enter_context(tc.manual_schedule())

        halves = [(c, first) for c in (Q, K, V) for first in (0, HALF)]

        q_planes = []
        q_slabs = []
        for h in range(2):
            q_planes.append(keep.tile([P, PASSES, HALF], U8, align_bytes=64, name="q_plane%d" % h))
            q_slabs.append(keep.tile([P, PASSES, 2 * HALF], U8, align_bytes=64, name="q_slab%d" % h))
        planes = {}
        slabs = {}
        for c in (K, V):
            planes[c] = keep.tile([P, PASSES, COMPONENT_COLS], U8, align_bytes=64, name="plane%d" % c)
            slabs[c] = keep.tile([P, PASSES, 2 * COMPONENT_COLS], U8, align_bytes=64, name="slab%d" % c)

        identity = keep.tile([P, P], F32, name="identity")
        make_identity(nc, identity[:])
        nc.vector.memset(q_planes[0][:].bitcast(I32), 0)
        nc.vector.memset(q_planes[1][:].bitcast(I32), 0)
        nc.gpsimd.memset(planes[K][:].bitcast(I32), 0)
        nc.gpsimd.memset(planes[V][:].bitcast(I32), 0)

        rope_sb = keep.tile([P, PARITIES, D], BF16, name="rope_sb")
        rope_rows = rope.rearrange("(m par) o d -> m (par o d)", par=PARITIES)
        nc.scalar.dma_start(
            out=rope_sb[:].rearrange("p par d -> p (par d)"),
            in_=rope_rows.unsqueeze(1).to_broadcast([POSITIONS // PARITIES, BATCH, PARITIES * D]),
        )

        x_by_parity = x.rearrange("b (m par) k -> par m b k", par=PARITIES)
        x_sb = keep.tile([P, PARITIES, HID], BF16, name="x_sb")

        for par in range(PARITIES):
            nc.sync.dma_start(out=x_sb[:, par, :], in_=x_by_parity[par])

        def load_scales(plane, first_col, passes):
            width = plane.shape[2]
            for r in range(4):
                nc.sync.dma_start(
                    out=plane[r:P:32, passes, :].bitcast(I32),
                    in_=qkv_w_scales[passes, r:16:4, first_col : first_col + width].rearrange("g q n -> q g n").bitcast(I32),
                )

        def load_words(slab, first_col, passes):
            width = slab.shape[2]
            nc.sync.dma_start(
                out=slab[:, passes, :].bitcast(I32),
                in_=qkv_w_words[passes, :, 2 * first_col : 2 * first_col + width].rearrange("g p n -> p g n").bitcast(I32),
            )

        def load_component(c):
            for g in range(0, PASSES, 2):
                load_words(slabs[c], c * COMPONENT_COLS, slice(g, g + 2))

        for h in range(2):
            load_scales(q_planes[h], h * HALF, slice(0, PASSES))
        for h in range(2):
            load_words(q_slabs[h], h * HALF, slice(0, PASSES))
        for c in (K, V):
            for g in range(0, PASSES, 2):
                load_scales(planes[c], c * COMPONENT_COLS, slice(g, g + 2))
        load_component(K)

        rope_pairs = rope_sb[:].rearrange("p par (j e) -> p par j e", e=2)
        cos2 = keep.tile([P, PARITIES, PAIRS, 2], F32, name="cos2")
        sin_pm = keep.tile([P, PARITIES, PAIRS, 2], F32, name="sin_pm")

        def make_tables():
            nc.scalar.copy(out=cos2[:], in_=rope_pairs[:, :, :, 0:1].to_broadcast([P, PARITIES, PAIRS, 2]))
            nc.scalar.mul(sin_pm[:, :, :, 0], rope_pairs[:, :, :, 1], -1.0)
            nc.scalar.copy(out=sin_pm[:, :, :, 1], in_=rope_pairs[:, :, :, 1])

        grouped = []
        x_codes = []
        x_scales = []
        for g in range(PASSES):
            grouped.append(keep.tile([P, PARITIES * P * PACK], BF16, align_bytes=64, name="grouped%d" % g))
            x_codes.append(keep.tile([P, PARITIES * P], U32, align_bytes=64, name="x_codes%d" % g))
            x_scales.append(keep.tile([P, PARITIES * P], U8, align_bytes=64, name="x_scales%d" % g))

        def turn_x(g, copy):
            xt = psum.tile([P, PARITIES, 2, P], F32, tag="bank", name="xt")
            for par in range(PARITIES):
                x_words = x_sb[:, par, :].bitcast(F32)
                for u in range(2):
                    nc.tensor.transpose(xt[:, par, u, :], x_words[:, 256 * g + u : 256 * (g + 1) : 2], identity[:])
            copy(
                out=grouped[g][:].bitcast(F32).rearrange("p (par t u) -> p par t u", par=PARITIES, u=2),
                in_=xt[:].rearrange("p par u t -> p par t u"),
            )

        def quantise_x(g):
            nc.vector.quantize_mx(out=x_codes[g][:].bitcast(FP8X4), scales=x_scales[g][:], in_=grouped[g][:])

        def multiply(acc, half, par, col, width, g):
            c, first = half
            if c == Q:
                plane, slab, start = q_planes[first // HALF], q_slabs[first // HALF], col
            else:
                plane, slab, start = planes[c], slabs[c], first + col
            nc.tensor.matmul_mx(
                out=acc,
                lhsT=x_codes[g][:, par * P : (par + 1) * P].bitcast(FP8X4),
                lhsT_scale=x_scales[g][:, par * P : (par + 1) * P],
                rhs=slab[:, g, 2 * start : 2 * (start + width)].bitcast(FP4X4),
                rhs_scale=plane[:, g, start : start + width],
                start=(g == 0),
                stop=(g == PASSES - 1),
            )

        def rope_products(acc, par, straight, crossed):
            nc.vector.tensor_tensor(
                out=straight,
                in0=acc[:].rearrange("p (h d) -> p h d", h=BANK_HEADS),
                in1=cos2[:, par, :, :].rearrange("p j e -> p (j e)").unsqueeze(1).to_broadcast([P, BANK_HEADS, D]),
                op=MULT,
            )
            nc.vector.tensor_tensor(
                out=crossed.rearrange("p h (j e) -> p h j e", e=2),
                in0=acc[:].rearrange("p (h j e) -> p h j e", h=BANK_HEADS, e=2)[:, :, :, ::-1],
                in1=sin_pm[:, par, :, :].unsqueeze(1).to_broadcast([P, BANK_HEADS, PAIRS, 2]),
                op=MULT,
            )

        def store(half, first_head, heads, result):
            head = half[1] // D + first_head
            out = outs[half[0]]
            start_dma = nc.scalar.dma_start if half[0] == V else nc.sync.dma_start
            for b in range(BATCH):
                start_dma(
                    out=out[b, head : head + heads, :, :].rearrange("h (m par) d -> m h (par d)", par=PARITIES),
                    in_=result[b:P:BATCH, first_head : first_head + heads, :, :].rearrange("p h par d -> p h (par d)"),
                )

        for g in range(PASSES):
            turn_x(g, nc.vector.tensor_copy if g % 2 else nc.scalar.copy)
            if g % 2:
                quantise_x(g - 1)
                quantise_x(g)
        make_tables()
        load_component(V)

        def store_head(c, head, result):
            nc.sync.dma_start(
                out=outs[c][:, head, :, :].rearrange("b (m par) d -> m b (par d)", par=PARITIES),
                in_=result.rearrange("p par d -> p (par d)"),
            )

        for half in halves:
            result = keep.tile([P, HALF_HEADS, PARITIES, D], F32, name="result%d_%d" % half)
            accs = {}
            if half == (K, 0):
                for col in range(0, HALF, BANK_COLS):
                    for par in range(PARITIES):
                        accs[col, par] = psum.tile([P, BANK_COLS], F32, tag="bank", name="acc")
                        for g in range(PASSES // 2):
                            multiply(accs[col, par][:], half, par, col, BANK_COLS, g)
            for col in range(0, HALF, BANK_COLS):
                first_head = col // D
                target = result[:, first_head : first_head + BANK_HEADS, :, :]
                if half == halves[-1] and col + BANK_COLS == HALF:
                    break
                if half[0] != V:
                    straight = work.tile([P, BANK_HEADS, PARITIES, D], F32, name="straight")
                    crossed = work.tile([P, BANK_HEADS, PARITIES, D], F32, name="crossed")
                for par in range(PARITIES):
                    acc = accs.get((col, par))
                    first_pass = PASSES // 2
                    if acc is None:
                        acc = psum.tile([P, BANK_COLS], F32, tag="bank", name="acc")
                        first_pass = 0
                    for g in range(first_pass, PASSES):
                        multiply(acc[:], half, par, col, BANK_COLS, g)
                    if half[0] == V:
                        nc.scalar.copy(out=target[:, :, par, :], in_=acc[:].rearrange("p (h d) -> p h d", h=BANK_HEADS))
                    else:
                        rope_products(acc, par, straight[:, :, par, :], crossed[:, :, par, :])
                if half[0] != V:
                    last_products = half == (K, HALF) and col + BANK_COLS == HALF
                    add = nc.vector.tensor_tensor if last_products else nc.gpsimd.tensor_tensor
                    add(
                        out=target.rearrange("p h par d -> p (h par d)"),
                        in0=straight[:].rearrange("p h par d -> p (h par d)"),
                        in1=crossed[:].rearrange("p h par d -> p (h par d)"),
                        op=ADD,
                    )
                if half[0] != Q:
                    store(half, first_head, BANK_HEADS, result)
            if half[0] == Q:
                store(half, 0, HALF_HEADS, result)
        for h in range(BANK_HEADS):
            acc = psum.tile([P, PARITIES, D], F32, tag="bank", name="acc")
            for par in range(PARITIES):
                for g in range(PASSES):
                    multiply(acc[:, par, :], halves[-1], par, HALF - BANK_COLS + h * D, D, g)
            copy = nc.vector.tensor_copy if h % 2 else nc.scalar.copy
            head_result = result[:, HALF_HEADS - BANK_HEADS + h, :, :]
            copy(out=head_result, in_=acc[:])
            store_head(V, HEADS - BANK_HEADS + h, head_result)
